import numpy as np
import ml_dtypes


def mxq(x, axis, fmt="e4m3"):
    dtype, down = {"e4m3": (ml_dtypes.float8_e4m3fn, 7), "e5m2": (ml_dtypes.float8_e5m2, 14)}[fmt]
    v = np.moveaxis(np.asarray(x, np.float32).astype(ml_dtypes.bfloat16).astype(np.float64), axis, -1)
    blocks = v.reshape(v.shape[:-1] + (-1, 32))
    amax = np.abs(blocks).max(-1, keepdims=True)
    byte = np.maximum(np.where(amax > 0, np.frexp(amax)[1] - 1 + 127, 0) - down, 1)
    scale = np.exp2(byte - 127.0)
    codes = (blocks / scale).astype(np.float32).astype(dtype).astype(np.float64)
    return np.moveaxis((codes * scale).reshape(v.shape), -1, axis)


WIDE = False


def mx_kscale(k):
    if not WIDE:
        return np.ones(k)
    levels = np.array([10, -10, 5, -5, 0])
    a = np.random.permutation(np.resize(levels, k // 512 * 4)).reshape(k // 512, 4)
    idx = np.arange(k)
    return np.exp2(a[idx // 512, idx % 128 // 32])


BF16 = ml_dtypes.bfloat16


def bf(x):
    return np.asarray(x, np.float32).astype(BF16)


def f64(x):
    return np.asarray(x).astype(np.float64)


B, N0, N1, N2, N3, T, K = 128, 512, 512, 512, 512, 1, 512
R = min(K, N0, N1)
R2 = min(R, T)
GS = 0.25


def setup_inputs():
    s, t = mx_kscale(R), mx_kscale(R)
    return {"S": bf(np.random.standard_normal((R, R, R2)) * s[:, None, None] * t[None, :, None]),
            "U0": bf(np.random.standard_normal((N1, R)) / np.sqrt(R) / s[None, :]),
            "U1": bf(np.random.standard_normal((N0, R)) * GS / np.sqrt(R) / t[None, :])}


def reference(S, U0, U1):
    w1 = mxq(f64(S).reshape(R, R * R2).T, 1, "e4m3") @ mxq(f64(U0).T, 0, "e4m3")
    w2 = mxq(w1.reshape(R, R2 * N1).T, 1, "e4m3") @ mxq(f64(U1).T, 0, "e4m3")
    return w2.reshape(R2, N1, N0)

@@ -1,0 +1,152 @@
+from contextlib import ExitStack
+
+import concourse.mybir as mybir
+from concourse.masks import make_identity
+
+BF16 = mybir.dt.bfloat16
+F32 = mybir.dt.float32
+U32 = mybir.dt.uint32
+U8 = mybir.dt.uint8
+FP8X4 = mybir.dt.float8_e4m3fn_x4
+
+P = 128
+PACK = 4
+DIM = 512
+HALF = DIM // 2
+BLOCKS = DIM // P
+RUN = 4
+
+FLOPS = 2 * 2 * DIM * DIM * DIM
+
+
+def copy_by_parity(nc, index, out, in_):
+    if index % 2 == 0:
+        nc.scalar.copy(out=out, in_=in_)
+    else:
+        nc.vector.tensor_copy(out=out, in_=in_)
+
+
+def load_factor(nc, pool, factor, name):
+    rows = pool.tile([P, 2, 2 * DIM], BF16, name=name)
+    for h in range(2):
+        nc.sync.dma_start(
+            out=rows[:, h, :],
+            in_=factor[h * HALF : (h + 1) * HALF, :].rearrange("(r b) k -> r (b k)", b=2),
+        )
+    return rows
+
+
+def quantise_factor(nc, pool, psum, rows, identity, name):
+    codes = pool.tile([P, DIM], U32, name=name + "_codes", align_bytes=64)
+    scales = pool.tile([P, DIM], U8, name=name + "_scales", align_bytes=64)
+    banks = []
+    for h in range(2):
+        words = rows[:, h, :].bitcast(F32)
+        bank = psum.tile([P, PACK, P], F32, tag="bank", name="%s_bank%d" % (name, h))
+        for s in range(PACK):
+            nc.tensor.transpose(bank[:, s, :], words[:, s * P : (s + 1) * P], identity[:])
+        banks.append(bank)
+    grouped = []
+    for h in range(2):
+        values = pool.tile([P, HALF * PACK], BF16, name="%s_grouped%d" % (name, h), align_bytes=64)
+        copy_by_parity(
+            nc,
+            h,
+            out=values[:].bitcast(F32).rearrange("w (r s) -> w r s", s=PACK),
+            in_=banks[h][:].rearrange("w s r -> w r s"),
+        )
+        grouped.append(values)
+    for h in range(2):
+        cols = slice(h * HALF, (h + 1) * HALF)
+        nc.vector.quantize_mx(
+            out=codes[:, cols].bitcast(FP8X4),
+            scales=scales[:, cols],
+            in_=grouped[h][:],
+        )
+    return codes, scales
+
+
+def tile_mtl_net_tf_pa_s_kernel(tc, S, U0, U1, out):
+    nc = tc.nc
+    with ExitStack() as ctx:
+        keep = ctx.enter_context(tc.tile_pool(name="keep", bufs=1))
+        psum = ctx.enter_context(tc.psum_pool(name="psum", bufs=8))
+
+        identity = keep.tile([P, P], F32)
+        make_identity(nc, identity[:])
+
+        s_rows = keep.tile([P, PACK, DIM], BF16)
+        nc.sync.dma_start(
+            out=s_rows[:].rearrange("w (u e) p -> w u (e p)", u=2),
+            in_=S.rearrange("(u w e) p r -> w u (e p r)", u=2, e=2),
+        )
+        u0_rows = load_factor(nc, keep, U0, "u0_rows")
+        u1_rows = load_factor(nc, keep, U1, "u1_rows")
+
+        s_grouped = keep.tile([P, DIM, PACK], BF16, align_bytes=64)
+        s_codes = keep.tile([P, DIM], U32, align_bytes=64)
+        s_scales = keep.tile([P, DIM], U8, align_bytes=64)
+        s_from = s_rows[:].rearrange("w t (u c i e) -> w u e c t i", u=2, i=RUN, e=2)
+        s_to = s_grouped[:].rearrange("w (u e c i) t -> w u e c t i", u=2, e=2, i=RUN)
+        for u in range(2):
+            for e in range(2):
+                copy_by_parity(nc, 1 - u, out=s_to[:, u, e], in_=s_from[:, u, e])
+        for u in range(2):
+            cols = slice(u * HALF, (u + 1) * HALF)
+            nc.vector.quantize_mx(
+                out=s_codes[:, cols].bitcast(FP8X4),
+                scales=s_scales[:, cols],
+                in_=s_grouped[:, cols, :].rearrange("w c t -> w (c t)"),
+            )
+
+        u0_codes, u0_scales = quantise_factor(nc, keep, psum, u0_rows, identity, "u0")
+        u1_codes, u1_scales = quantise_factor(nc, keep, psum, u1_rows, identity, "u1")
+
+        w1_banks = []
+        for jb in range(BLOCKS):
+            j_cols = slice(jb * P, (jb + 1) * P)
+            w1_bank = psum.tile([P, PACK, P], F32, tag="bank", name="w1_bank%d" % jb)
+            for t in range(PACK):
+                p_cols = slice(t * P, (t + 1) * P)
+                nc.tensor.matmul_mx(
+                    out=w1_bank[:, t, :],
+                    lhsT=s_codes[:, p_cols].bitcast(FP8X4),
+                    lhsT_scale=s_scales[:, p_cols],
+                    rhs=u0_codes[:, j_cols].bitcast(FP8X4),
+                    rhs_scale=u0_scales[:, j_cols],
+                    start=True,
+                    stop=True,
+                )
+            w1_banks.append(w1_bank)
+
+        w1_codes = keep.tile([P, DIM], U32, align_bytes=64)
+        w1_scales = keep.tile([P, DIM], U8, align_bytes=64)
+        for pair in range(BLOCKS // 2):
+            w1_grouped = []
+            for jb in (2 * pair, 2 * pair + 1):
+                grouped = keep.tile([P, P, PACK], BF16, name="w1_grouped%d" % jb, align_bytes=64)
+                copy_by_parity(nc, jb, out=grouped[:], in_=w1_banks[jb][:].rearrange("c t j -> c j t"))
+                w1_grouped.append(grouped)
+            for jb in (2 * pair, 2 * pair + 1):
+                j_cols = slice(jb * P, (jb + 1) * P)
+                nc.vector.quantize_mx(
+                    out=w1_codes[:, j_cols].bitcast(FP8X4),
+                    scales=w1_scales[:, j_cols],
+                    in_=w1_grouped[jb % 2][:].rearrange("c j t -> c (j t)"),
+                )
+
+        for jb in range(BLOCKS):
+            j_cols = slice(jb * P, (jb + 1) * P)
+            out_bank = psum.tile([P, DIM], F32, tag="bank", name="out_bank%d" % jb)
+            nc.tensor.matmul_mx(
+                out=out_bank[:],
+                lhsT=w1_codes[:, j_cols].bitcast(FP8X4),
+                lhsT_scale=w1_scales[:, j_cols],
+                rhs=u1_codes[:].bitcast(FP8X4),
+                rhs_scale=u1_scales[:],
+                start=True,
+                stop=True,
+            )
+            out_rows = keep.tile([P, DIM], F32, name="out_rows%d" % jb)
+            copy_by_parity(nc, jb, out=out_rows[:], in_=out_bank[:])
+            nc.sync.dma_start(out=out[0, j_cols, :], in_=out_rows[:])

@@ -15,6 +15,7 @@ DIM = 512
 HALF = DIM // 2
 BLOCKS = DIM // P
 RUN = 4
+WARM_MATMULS = 6
 
 FLOPS = 2 * 2 * DIM * DIM * DIM
 
@@ -74,6 +75,10 @@ def tile_mtl_net_tf_pa_s_kernel(tc, S, U0, U1, out):
 
         identity = keep.tile([P, P], F32)
         make_identity(nc, identity[:])
+
+        idle_bank = psum.tile([P, P], F32, tag="bank")
+        for n in range(WARM_MATMULS):
+            nc.tensor.matmul(out=idle_bank[:], lhsT=identity[:], rhs=identity[:], start=True, stop=True)
 
         s_rows = keep.tile([P, PACK, DIM], BF16)
         nc.sync.dma_start(

@@ -20,11 +20,15 @@ WARM_MATMULS = 6
 FLOPS = 2 * 2 * DIM * DIM * DIM
 
 
-def copy_by_parity(nc, index, out, in_):
-    if index % 2 == 0:
-        nc.scalar.copy(out=out, in_=in_)
-    else:
+def empty_bank(nc, on_vector, out, in_):
+    if on_vector:
         nc.vector.tensor_copy(out=out, in_=in_)
+    else:
+        nc.scalar.copy(out=out, in_=in_)
+
+
+def quantise(nc, codes, scales, cols, values):
+    nc.vector.quantize_mx(out=codes[:, cols].bitcast(FP8X4), scales=scales[:, cols], in_=values)
 
 
 def load_factor(nc, pool, factor, name):
@@ -37,7 +41,7 @@ def load_factor(nc, pool, factor, name):
     return rows
 
 
-def quantise_factor(nc, pool, psum, rows, identity, name):
+def quantise_factor(nc, pool, psum, rows, identity, vector_takes_last, name):
     codes = pool.tile([P, DIM], U32, name=name + "_codes", align_bytes=64)
     scales = pool.tile([P, DIM], U8, name=name + "_scales", align_bytes=64)
     banks = []
@@ -50,35 +54,28 @@ def quantise_factor(nc, pool, psum, rows, identity, name):
     grouped = []
     for h in range(2):
         values = pool.tile([P, HALF * PACK], BF16, name="%s_grouped%d" % (name, h), align_bytes=64)
-        copy_by_parity(
+        empty_bank(
             nc,
-            h,
+            vector_takes_last and h == 1,
             out=values[:].bitcast(F32).rearrange("w (r s) -> w r s", s=PACK),
             in_=banks[h][:].rearrange("w s r -> w r s"),
         )
         grouped.append(values)
-    for h in range(2):
-        cols = slice(h * HALF, (h + 1) * HALF)
-        nc.vector.quantize_mx(
-            out=codes[:, cols].bitcast(FP8X4),
-            scales=scales[:, cols],
-            in_=grouped[h][:],
-        )
+        if h == 1:
+            quantise(nc, codes, scales, slice(0, HALF), grouped[0][:])
+    quantise(nc, codes, scales, slice(HALF, DIM), grouped[1][:])
     return codes, scales
 
 
 def tile_mtl_net_tf_pa_s_kernel(tc, S, U0, U1, out):
     nc = tc.nc
     with ExitStack() as ctx:
+        ctx.enter_context(tc.manual_schedule())
         keep = ctx.enter_context(tc.tile_pool(name="keep", bufs=1))
         psum = ctx.enter_context(tc.psum_pool(name="psum", bufs=8))
 
         identity = keep.tile([P, P], F32)
         make_identity(nc, identity[:])
-
-        idle_bank = psum.tile([P, P], F32, tag="bank")
-        for n in range(WARM_MATMULS):
-            nc.tensor.matmul(out=idle_bank[:], lhsT=identity[:], rhs=identity[:], start=True, stop=True)
 
         s_rows = keep.tile([P, PACK, DIM], BF16)
         nc.sync.dma_start(
@@ -88,24 +85,25 @@ def tile_mtl_net_tf_pa_s_kernel(tc, S, U0, U1, out):
         u0_rows = load_factor(nc, keep, U0, "u0_rows")
         u1_rows = load_factor(nc, keep, U1, "u1_rows")
 
+        idle_bank = psum.tile([P, P], F32, tag="bank")
+        for n in range(WARM_MATMULS):
+            nc.tensor.matmul(out=idle_bank[:], lhsT=identity[:], rhs=identity[:], start=True, stop=True)
+
         s_grouped = keep.tile([P, DIM, PACK], BF16, align_bytes=64)
         s_codes = keep.tile([P, DIM], U32, align_bytes=64)
         s_scales = keep.tile([P, DIM], U8, align_bytes=64)
         s_from = s_rows[:].rearrange("w t (u c i e) -> w u e c t i", u=2, i=RUN, e=2)
         s_to = s_grouped[:].rearrange("w (u e c i) t -> w u e c t i", u=2, e=2, i=RUN)
+        s_values = s_grouped[:].rearrange("w c t -> w (c t)")
         for u in range(2):
             for e in range(2):
-                copy_by_parity(nc, 1 - u, out=s_to[:, u, e], in_=s_from[:, u, e])
-        for u in range(2):
-            cols = slice(u * HALF, (u + 1) * HALF)
-            nc.vector.quantize_mx(
-                out=s_codes[:, cols].bitcast(FP8X4),
-                scales=s_scales[:, cols],
-                in_=s_grouped[:, cols, :].rearrange("w c t -> w (c t)"),
-            )
+                nc.vector.tensor_copy(out=s_to[:, u, e], in_=s_from[:, u, e])
+            if u == 1:
+                quantise(nc, s_codes, s_scales, slice(0, HALF), s_values[:, 0 : HALF * PACK])
+        quantise(nc, s_codes, s_scales, slice(HALF, DIM), s_values[:, HALF * PACK : DIM * PACK])
 
-        u0_codes, u0_scales = quantise_factor(nc, keep, psum, u0_rows, identity, "u0")
-        u1_codes, u1_scales = quantise_factor(nc, keep, psum, u1_rows, identity, "u1")
+        u0_codes, u0_scales = quantise_factor(nc, keep, psum, u0_rows, identity, False, "u0")
+        u1_codes, u1_scales = quantise_factor(nc, keep, psum, u1_rows, identity, True, "u1")
 
         w1_banks = []
         for jb in range(BLOCKS):
@@ -126,19 +124,14 @@ def tile_mtl_net_tf_pa_s_kernel(tc, S, U0, U1, out):
 
         w1_codes = keep.tile([P, DIM], U32, align_bytes=64)
         w1_scales = keep.tile([P, DIM], U8, align_bytes=64)
-        for pair in range(BLOCKS // 2):
-            w1_grouped = []
-            for jb in (2 * pair, 2 * pair + 1):
-                grouped = keep.tile([P, P, PACK], BF16, name="w1_grouped%d" % jb, align_bytes=64)
-                copy_by_parity(nc, jb, out=grouped[:], in_=w1_banks[jb][:].rearrange("c t j -> c j t"))
-                w1_grouped.append(grouped)
-            for jb in (2 * pair, 2 * pair + 1):
-                j_cols = slice(jb * P, (jb + 1) * P)
-                nc.vector.quantize_mx(
-                    out=w1_codes[:, j_cols].bitcast(FP8X4),
-                    scales=w1_scales[:, j_cols],
-                    in_=w1_grouped[jb % 2][:].rearrange("c j t -> c (j t)"),
-                )
+        w1_grouped = []
+        for jb in range(BLOCKS):
+            values = keep.tile([P, P, PACK], BF16, name="w1_grouped%d" % jb, align_bytes=64)
+            empty_bank(nc, jb == BLOCKS - 1, out=values[:], in_=w1_banks[jb][:].rearrange("c t j -> c j t"))
+            w1_grouped.append(values[:].rearrange("c j t -> c (j t)"))
+            if jb > 0:
+                quantise(nc, w1_codes, w1_scales, slice((jb - 1) * P, jb * P), w1_grouped[jb - 1])
+        quantise(nc, w1_codes, w1_scales, slice(DIM - P, DIM), w1_grouped[BLOCKS - 1])
 
         for jb in range(BLOCKS):
             j_cols = slice(jb * P, (jb + 1) * P)
@@ -153,5 +146,5 @@ def tile_mtl_net_tf_pa_s_kernel(tc, S, U0, U1, out):
                 stop=True,
             )
             out_rows = keep.tile([P, DIM], F32, name="out_rows%d" % jb)
-            copy_by_parity(nc, jb, out=out_rows[:], in_=out_bank[:])
+            empty_bank(nc, jb == BLOCKS - 1, out=out_rows[:], in_=out_bank[:])
             nc.sync.dma_start(out=out[0, j_cols, :], in_=out_rows[:])

@@ -41,16 +41,21 @@ def load_factor(nc, pool, factor, name):
     return rows
 
 
-def quantise_factor(nc, pool, psum, rows, identity, vector_takes_last, name):
+def idle_matmul(nc, idle_bank, identity):
+    nc.tensor.matmul(out=idle_bank[:], lhsT=identity[:], rhs=identity[:], start=True, stop=True)
+
+
+def transpose_half(nc, psum, rows, h, identity, name):
+    words = rows[:, h, :].bitcast(F32)
+    bank = psum.tile([P, PACK, P], F32, tag="bank", name="%s_bank%d" % (name, h))
+    for s in range(PACK):
+        nc.tensor.transpose(bank[:, s, :], words[:, s * P : (s + 1) * P], identity[:])
+    return bank
+
+
+def quantise_factor(nc, pool, banks, vector_takes_last, name):
     codes = pool.tile([P, DIM], U32, name=name + "_codes", align_bytes=64)
     scales = pool.tile([P, DIM], U8, name=name + "_scales", align_bytes=64)
-    banks = []
-    for h in range(2):
-        words = rows[:, h, :].bitcast(F32)
-        bank = psum.tile([P, PACK, P], F32, tag="bank", name="%s_bank%d" % (name, h))
-        for s in range(PACK):
-            nc.tensor.transpose(bank[:, s, :], words[:, s * P : (s + 1) * P], identity[:])
-        banks.append(bank)
     grouped = []
     for h in range(2):
         values = pool.tile([P, HALF * PACK], BF16, name="%s_grouped%d" % (name, h), align_bytes=64)
@@ -87,7 +92,17 @@ def tile_mtl_net_tf_pa_s_kernel(tc, S, U0, U1, out):
 
         idle_bank = psum.tile([P, P], F32, tag="bank")
         for n in range(WARM_MATMULS):
-            nc.tensor.matmul(out=idle_bank[:], lhsT=identity[:], rhs=identity[:], start=True, stop=True)
+            idle_matmul(nc, idle_bank, identity)
+
+        u0_banks = []
+        u1_banks = []
+        for h in range(2):
+            u0_banks.append(transpose_half(nc, psum, u0_rows, h, identity, "u0"))
+            idle_matmul(nc, idle_bank, identity)
+        for h in range(2):
+            u1_banks.append(transpose_half(nc, psum, u1_rows, h, identity, "u1"))
+            if h == 0:
+                idle_matmul(nc, idle_bank, identity)
 
         s_grouped = keep.tile([P, DIM, PACK], BF16, align_bytes=64)
         s_codes = keep.tile([P, DIM], U32, align_bytes=64)
@@ -102,8 +117,8 @@ def tile_mtl_net_tf_pa_s_kernel(tc, S, U0, U1, out):
                 quantise(nc, s_codes, s_scales, slice(0, HALF), s_values[:, 0 : HALF * PACK])
         quantise(nc, s_codes, s_scales, slice(HALF, DIM), s_values[:, HALF * PACK : DIM * PACK])
 
-        u0_codes, u0_scales = quantise_factor(nc, keep, psum, u0_rows, identity, False, "u0")
-        u1_codes, u1_scales = quantise_factor(nc, keep, psum, u1_rows, identity, True, "u1")
+        u0_codes, u0_scales = quantise_factor(nc, keep, u0_banks, False, "u0")
+        u1_codes, u1_scales = quantise_factor(nc, keep, u1_banks, True, "u1")
 
         w1_banks = []
         for jb in range(BLOCKS):

from contextlib import ExitStack

import concourse.mybir as mybir
from concourse.masks import make_identity

BF16 = mybir.dt.bfloat16
F32 = mybir.dt.float32
U32 = mybir.dt.uint32
U8 = mybir.dt.uint8
FP8X4 = mybir.dt.float8_e4m3fn_x4

P = 128
PACK = 4
DIM = 512
HALF = DIM // 2
BLOCKS = DIM // P
RUN = 4
WARM_MATMULS = 6

FLOPS = 2 * 2 * DIM * DIM * DIM


def empty_bank(nc, on_vector, out, in_):
    if on_vector:
        nc.vector.tensor_copy(out=out, in_=in_)
    else:
        nc.scalar.copy(out=out, in_=in_)


def quantise(nc, codes, scales, cols, values):
    nc.vector.quantize_mx(out=codes[:, cols].bitcast(FP8X4), scales=scales[:, cols], in_=values)


def load_factor(nc, pool, factor, name):
    rows = pool.tile([P, 2, 2 * DIM], BF16, name=name)
    for h in range(2):
        nc.sync.dma_start(
            out=rows[:, h, :],
            in_=factor[h * HALF : (h + 1) * HALF, :].rearrange("(r b) k -> r (b k)", b=2),
        )
    return rows


def idle_matmul(nc, idle_bank, identity):
    nc.tensor.matmul(out=idle_bank[:], lhsT=identity[:], rhs=identity[:], start=True, stop=True)


def transpose_half(nc, psum, rows, h, identity, name):
    words = rows[:, h, :].bitcast(F32)
    bank = psum.tile([P, PACK, P], F32, tag="bank", name="%s_bank%d" % (name, h))
    for s in range(PACK):
        nc.tensor.transpose(bank[:, s, :], words[:, s * P : (s + 1) * P], identity[:])
    return bank


def quantise_factor(nc, pool, banks, vector_takes_last, name):
    codes = pool.tile([P, DIM], U32, name=name + "_codes", align_bytes=64)
    scales = pool.tile([P, DIM], U8, name=name + "_scales", align_bytes=64)
    grouped = []
    for h in range(2):
        values = pool.tile([P, HALF * PACK], BF16, name="%s_grouped%d" % (name, h), align_bytes=64)
        empty_bank(
            nc,
            vector_takes_last and h == 1,
            out=values[:].bitcast(F32).rearrange("w (r s) -> w r s", s=PACK),
            in_=banks[h][:].rearrange("w s r -> w r s"),
        )
        grouped.append(values)
        if h == 1:
            quantise(nc, codes, scales, slice(0, HALF), grouped[0][:])
    quantise(nc, codes, scales, slice(HALF, DIM), grouped[1][:])
    return codes, scales


def tile_mtl_net_tf_pa_s_kernel(tc, S, U0, U1, out):
    nc = tc.nc
    with ExitStack() as ctx:
        ctx.enter_context(tc.manual_schedule())
        keep = ctx.enter_context(tc.tile_pool(name="keep", bufs=1))
        psum = ctx.enter_context(tc.psum_pool(name="psum", bufs=8))

        identity = keep.tile([P, P], F32)
        make_identity(nc, identity[:])

        s_rows = keep.tile([P, PACK, DIM], BF16)
        nc.sync.dma_start(
            out=s_rows[:].rearrange("w (u e) p -> w u (e p)", u=2),
            in_=S.rearrange("(u w e) p r -> w u (e p r)", u=2, e=2),
        )
        u0_rows = load_factor(nc, keep, U0, "u0_rows")
        u1_rows = load_factor(nc, keep, U1, "u1_rows")

        idle_bank = psum.tile([P, P], F32, tag="bank")
        for n in range(WARM_MATMULS):
            idle_matmul(nc, idle_bank, identity)

        u0_banks = []
        u1_banks = []
        for h in range(2):
            u0_banks.append(transpose_half(nc, psum, u0_rows, h, identity, "u0"))
            idle_matmul(nc, idle_bank, identity)
        for h in range(2):
            u1_banks.append(transpose_half(nc, psum, u1_rows, h, identity, "u1"))
            if h == 0:
                idle_matmul(nc, idle_bank, identity)

        s_grouped = keep.tile([P, DIM, PACK], BF16, align_bytes=64)
        s_codes = keep.tile([P, DIM], U32, align_bytes=64)
        s_scales = keep.tile([P, DIM], U8, align_bytes=64)
        s_from = s_rows[:].rearrange("w t (u c i e) -> w u e c t i", u=2, i=RUN, e=2)
        s_to = s_grouped[:].rearrange("w (u e c i) t -> w u e c t i", u=2, e=2, i=RUN)
        s_values = s_grouped[:].rearrange("w c t -> w (c t)")
        for u in range(2):
            for e in range(2):
                nc.vector.tensor_copy(out=s_to[:, u, e], in_=s_from[:, u, e])
            if u == 1:
                quantise(nc, s_codes, s_scales, slice(0, HALF), s_values[:, 0 : HALF * PACK])
        quantise(nc, s_codes, s_scales, slice(HALF, DIM), s_values[:, HALF * PACK : DIM * PACK])

        u0_codes, u0_scales = quantise_factor(nc, keep, u0_banks, False, "u0")
        u1_codes, u1_scales = quantise_factor(nc, keep, u1_banks, True, "u1")

        w1_banks = []
        for jb in range(BLOCKS):
            j_cols = slice(jb * P, (jb + 1) * P)
            w1_bank = psum.tile([P, PACK, P], F32, tag="bank", name="w1_bank%d" % jb)
            for t in range(PACK):
                p_cols = slice(t * P, (t + 1) * P)
                nc.tensor.matmul_mx(
                    out=w1_bank[:, t, :],
                    lhsT=s_codes[:, p_cols].bitcast(FP8X4),
                    lhsT_scale=s_scales[:, p_cols],
                    rhs=u0_codes[:, j_cols].bitcast(FP8X4),
                    rhs_scale=u0_scales[:, j_cols],
                    start=True,
                    stop=True,
                )
            w1_banks.append(w1_bank)

        w1_codes = keep.tile([P, DIM], U32, align_bytes=64)
        w1_scales = keep.tile([P, DIM], U8, align_bytes=64)
        w1_grouped = []
        for jb in range(BLOCKS):
            values = keep.tile([P, P, PACK], BF16, name="w1_grouped%d" % jb, align_bytes=64)
            empty_bank(nc, jb == BLOCKS - 1, out=values[:], in_=w1_banks[jb][:].rearrange("c t j -> c j t"))
            w1_grouped.append(values[:].rearrange("c j t -> c (j t)"))
            if jb > 0:
                quantise(nc, w1_codes, w1_scales, slice((jb - 1) * P, jb * P), w1_grouped[jb - 1])
        quantise(nc, w1_codes, w1_scales, slice(DIM - P, DIM), w1_grouped[BLOCKS - 1])

        for jb in range(BLOCKS):
            j_cols = slice(jb * P, (jb + 1) * P)
            out_bank = psum.tile([P, DIM], F32, tag="bank", name="out_bank%d" % jb)
            nc.tensor.matmul_mx(
                out=out_bank[:],
                lhsT=w1_codes[:, j_cols].bitcast(FP8X4),
                lhsT_scale=w1_scales[:, j_cols],
                rhs=u1_codes[:].bitcast(FP8X4),
                rhs_scale=u1_scales[:],
                start=True,
                stop=True,
            )
            out_rows = keep.tile([P, DIM], F32, name="out_rows%d" % jb)
            empty_bank(nc, jb == BLOCKS - 1, out=out_rows[:], in_=out_bank[:])
            nc.sync.dma_start(out=out[0, j_cols, :], in_=out_rows[:])
